import numpy as np
import ml_dtypes


def mxq(x, axis, fmt="e4m3"):
    dtype, down = {"e4m3": (ml_dtypes.float8_e4m3fn, 7), "e5m2": (ml_dtypes.float8_e5m2, 14)}[fmt]
    v = np.moveaxis(np.asarray(x, np.float32).astype(ml_dtypes.bfloat16).astype(np.float64), axis, -1)
    blocks = v.reshape(v.shape[:-1] + (-1, 32))
    amax = np.abs(blocks).max(-1, keepdims=True)
    byte = np.maximum(np.where(amax > 0, np.frexp(amax)[1] - 1 + 127, 0) - down, 1)
    scale = np.exp2(byte - 127.0)
    codes = (blocks / scale).astype(np.float32).astype(dtype).astype(np.float64)
    return np.moveaxis((codes * scale).reshape(v.shape), -1, axis)


WIDE = False


def mx_kscale(k):
    if not WIDE:
        return np.ones(k)
    levels = np.array([10, -10, 5, -5, 0])
    if k % 512:
        return np.exp2(np.random.permutation(np.resize(levels, k // 32))).repeat(32)
    a = np.empty((k // 512, 16))
    for p in range(k // 512):
        a[p, :8] = np.random.permutation(np.resize(levels, 8))
        for g in range(8):
            far = levels[np.abs(levels - a[p, g]) >= 10]
            a[p, g + 8] = far[np.random.randint(len(far))]
    return np.exp2(a.ravel()).repeat(32)


BF16 = ml_dtypes.bfloat16


def bf(x):
    return np.asarray(x, np.float32).astype(BF16)


def f64(x):
    return np.asarray(x).astype(np.float64)


B, S, D = 128, 16, 512
EPS = 1e-9


def layernorm(x, gain, bias_):
    mu = x.mean(-1, keepdims=True)
    sd = x.std(-1, keepdims=True)
    return gain * (x - mu) / (sd + EPS) + bias_


def setup_inputs():
    s, t = mx_kscale(D), mx_kscale(D)
    return {
        "c_att": bf(np.random.standard_normal((B, S, D)) * 0.4 * s),
        "mlp_kernel_1": bf(np.random.standard_normal((D, D)) / np.sqrt(D) / s[:, None]),
        "mlp_kernel_2": bf(np.random.standard_normal((D, D)) / np.sqrt(D) / t[:, None]),
        "mlp_gain_1": bf((1.0 + 0.1 * np.random.standard_normal(D)) * t),
        "mlp_gain_2": bf(1.0 + 0.1 * np.random.standard_normal(D)),
        "mlp_bias_1": bf(0.1 * np.random.standard_normal(D) * t),
        "mlp_bias_2": bf(0.1 * np.random.standard_normal(D)),
    }


def reference(c_att, mlp_kernel_1, mlp_kernel_2, mlp_gain_1, mlp_gain_2, mlp_bias_1, mlp_bias_2):
    y1 = mxq(f64(c_att), 2, "e4m3") @ mxq(f64(mlp_kernel_1), 0, "e4m3")
    h = np.maximum(layernorm(y1, f64(mlp_gain_1), f64(mlp_bias_1)), 0.0)
    y2 = mxq(h, 2, "e4m3") @ mxq(f64(mlp_kernel_2), 0, "e4m3")
    return layernorm(y2, f64(mlp_gain_2), f64(mlp_bias_2))

@@ -1,0 +1,448 @@
+from contextlib import ExitStack
+
+import concourse.mybir as mybir
+from concourse.masks import make_identity
+
+F32 = mybir.dt.float32
+BF16 = mybir.dt.bfloat16
+U32 = mybir.dt.uint32
+U8 = mybir.dt.uint8
+FP8X4 = mybir.dt.float8_e4m3fn_x4
+ACT = mybir.ActivationFunctionType
+ALU = mybir.AluOpType
+
+P = 128
+S = 16
+D = 512
+EPS = 1e-9
+NP = S // 2
+FLOPS = 2 * 2 * (P * S) * D * D
+
+PINNED = True
+V_STATS = (0, 1)
+
+
+def tile_rlstmcell_pa_kernel(
+    tc, c_att, mlp_kernel_1, mlp_kernel_2, mlp_gain_1, mlp_gain_2, mlp_bias_1, mlp_bias_2, out
+):
+    nc = tc.nc
+    with ExitStack() as ctx:
+        const = ctx.enter_context(tc.tile_pool(name="const", bufs=1))
+        work = ctx.enter_context(tc.tile_pool(name="work", bufs=3))
+        small = ctx.enter_context(tc.tile_pool(name="small", bufs=5))
+        psum = ctx.enter_context(tc.psum_pool(name="psum", bufs=2))
+        if PINNED:
+            ctx.enter_context(tc.manual_schedule())
+
+        def bank(tag, name):
+            return psum.tile([P, D], F32, tag=tag, bufs=(4 if tag == "zt" else 2), name=name)
+
+        warm_in = const.tile([P, 1], F32)
+        warm_out = const.tile([P, 1], F32)
+        nc.vector.memset(warm_in[:], 1.0)
+        ident = const.tile([P, P], F32)
+        make_identity(nc, ident[:])
+
+        gb1raw = const.tile([P, 2, 16], BF16)
+        nc.scalar.dma_start(out=gb1raw[:, 0, 0:4], in_=mlp_gain_1.rearrange("(p t) -> p t", t=4))
+        nc.scalar.dma_start(out=gb1raw[:, 1, 0:4], in_=mlp_bias_1.rearrange("(p t) -> p t", t=4))
+        nc.scalar.sqrt(out=warm_out[:], in_=warm_in[:])
+        w1raw = const.tile([P, 4, D], BF16)
+        nc.sync.dma_start(out=w1raw[:], in_=mlp_kernel_1.rearrange("(p j) c -> p j c", j=4))
+        x_all = const.tile([P, S, D], BF16)
+        for lo, hi in ((0, 2), (2, 4), (4, 8), (8, 12), (12, 16)):
+            nc.sync.dma_start(out=x_all[:, lo:hi, :], in_=c_att[:, lo:hi, :])
+        w2raw = const.tile([P, 4, D], BF16)
+        nc.sync.dma_start(out=w2raw[:], in_=mlp_kernel_2.rearrange("(p j) c -> p j c", j=4))
+        gb2 = const.tile([P, 2, D], BF16)
+        nc.sync.dma_start(out=gb2[:, 0, :], in_=mlp_gain_2.partition_broadcast(P))
+        nc.sync.dma_start(out=gb2[:, 1, :], in_=mlp_bias_2.partition_broadcast(P))
+        x_words = x_all[:].rearrange("p s d -> p (s d)").bitcast(F32)
+
+        live = {}
+
+        gb1 = const.tile([P, 8], F32)
+
+        def gains1_cast():
+            nc.vector.tensor_copy(out=gb1[:].rearrange("p (a t) -> p a t", a=2), in_=gb1raw[:, :, 0:4])
+
+        wg = {}
+        wcodes = {}
+        wscales = {}
+        for label in ("w1", "w2"):
+            wg[label] = const.tile([P, D, 4], BF16, align_bytes=64, name=label + "_grouped")
+            wcodes[label] = const.tile([P, D], U32, align_bytes=64, name=label + "_codes")
+            wscales[label] = const.tile([P, D], U8, align_bytes=64, name=label + "_scales")
+        xcodes = const.tile([P, S * P], U32, align_bytes=64)
+        xscales = const.tile([P, S * P], U8, align_bytes=64)
+        hcodes = const.tile([P, S * P], U32, align_bytes=64)
+        hscales = const.tile([P, S * P], U8, align_bytes=64)
+
+        def regroup_weight(label, raw, lo, hi):
+            nc.vector.tensor_copy(
+                out=wg[label][:, lo:hi, :].rearrange("p (c i) t -> p c t i", i=4),
+                in_=raw[:, :, lo:hi].rearrange("p t (c i) -> p c t i", i=4),
+            )
+
+        def quantise_weight(label, lo, hi):
+            nc.vector.quantize_mx(
+                out=wcodes[label][:, lo:hi].bitcast(FP8X4),
+                scales=wscales[label][:, lo:hi],
+                in_=wg[label][:, lo:hi, :].rearrange("p c t -> p (c t)"),
+            )
+
+        def ok(q):
+            return 0 <= q < NP
+
+        def mx(dst, codes, scales, s, label):
+            nc.tensor.matmul_mx(
+                out=dst[:],
+                lhsT=codes[:, s * P : (s + 1) * P].bitcast(FP8X4),
+                lhsT_scale=scales[:, s * P : (s + 1) * P],
+                rhs=wcodes[label][:].bitcast(FP8X4),
+                rhs_scale=wscales[label][:],
+                start=True,
+                stop=True,
+            )
+
+        def XT(q):
+            if not ok(q):
+                return
+            xt = bank("zt", "xt")
+            live["xt", q] = xt
+            for i in range(2):
+                for u in range(2):
+                    col = (2 * q + i) * 256 + u
+                    nc.tensor.transpose(
+                        out=xt[:, (2 * i + u) * P : (2 * i + u + 1) * P],
+                        in_=x_words[:, col : col + 2 * P - 1 : 2],
+                        identity=ident[:],
+                    )
+
+        def XC(q):
+            if not ok(q):
+                return
+            xg = work.tile([P, 2 * D], BF16, align_bytes=64, tag="xg", bufs=4, name="xg")
+            live["xg", q] = xg
+            nc.scalar.copy(
+                out=xg[:].bitcast(F32).rearrange("p (i k u) -> p i k u", i=2, u=2),
+                in_=live["xt", q][:].rearrange("p (i u k) -> p i k u", i=2, u=2),
+            )
+
+        def XQ(q):
+            if not ok(q):
+                return
+            cols = slice(2 * q * P, (2 * q + 2) * P)
+            nc.vector.quantize_mx(out=xcodes[:, cols].bitcast(FP8X4), scales=xscales[:, cols], in_=live["xg", q][:])
+
+        def MS(q, i):
+            if ok(q):
+                live["ys", q, i] = bank("ys", "ys")
+                mx(live["ys", q, i], xcodes, xscales, 2 * q + i, "w1")
+
+        def MN(q, i):
+            if ok(q):
+                live["yn", q, i] = bank("yn", "yn")
+                mx(live["yn", q, i], xcodes, xscales, 2 * q + i, "w1")
+
+        def moments(key, q, i, src):
+            if i == 0:
+                live[key + "st", q] = small.tile([P, 2, 6], F32, tag=key + "st", name=key + "st")
+            nc.vector.bn_stats(out=live[key + "st", q][:, i, :], in_=live[src, q, i][:])
+
+        def aggregate(key, q, i):
+            if i == 0:
+                live[key + "mv", q] = small.tile([P, 2, 2], F32, tag=key + "mv", name=key + "mv")
+            nc.vector.bn_aggr(out=live[key + "mv", q][:, i, :], in_=live[key + "st", q][:, i, :])
+
+        def BN(q, i):
+            if ok(q):
+                moments("a", q, i, "ys")
+
+        def AG(q, i):
+            if ok(q):
+                aggregate("a", q, i)
+
+        def root(key, q, src_ap, divisor):
+            sd = small.tile([P, 2], F32, tag=key + "sd", name=key + "sd")
+            live[key + "sd", q] = sd
+            nc.scalar.activation(out=sd[:], in_=src_ap, func=ACT.Sqrt, scale=1.0 / divisor)
+
+        def add_eps(key, q):
+            sde = small.tile([P, 2], F32, tag=key + "sde", name=key + "sde")
+            live[key + "sde", q] = sde
+            nc.vector.tensor_scalar_add(out=sde[:], in0=live[key + "sd", q][:], scalar1=EPS)
+
+        def invert(key, q):
+            r = small.tile([P, 2], F32, tag=key + "r", name=key + "r")
+            live[key + "r", q] = r
+            nc.vector.reciprocal(out=r[:], in_=live[key + "sde", q][:])
+
+        def SQ(q):
+            if ok(q):
+                root("a", q, live["amv", q][:, :, 1], 1)
+
+        def E1(q):
+            if ok(q):
+                add_eps("a", q)
+
+        def R1(q):
+            if ok(q):
+                invert("a", q)
+
+        def N1(q):
+            if not ok(q):
+                return
+            nmr = small.tile([P, 2], F32, tag="anmr", name="anmr")
+            live["anmr", q] = nmr
+            nc.vector.scalar_tensor_tensor(
+                out=nmr[:], in0=live["amv", q][:, :, 0], scalar=-1.0, in1=live["ar", q][:], op0=ALU.mult, op1=ALU.mult
+            )
+
+        def NR(q, i):
+            if not ok(q):
+                return
+            if i == 0:
+                live["z", q] = work.tile([P, 2, D], F32, tag="z", name="z")
+            nc.scalar.activation(
+                out=live["z", q][:, i, :].rearrange("p (t m) -> p t m", t=4),
+                in_=live["yn", q, i][:].rearrange("p (m t) -> p t m", t=4),
+                func=ACT.Identity,
+                bias=live["anmr", q][:, i : i + 1],
+                scale=live["ar", q][:, i : i + 1],
+            )
+
+        def ZT(q):
+            if not ok(q):
+                return
+            zts = [bank("zt", "zt"), bank("zt", "zt")]
+            live["zt", q] = zts
+            for i in range(2):
+                for j in range(4):
+                    col = (2 * (j % 2) + i) * P
+                    nc.tensor.transpose(
+                        out=zts[j // 2][:, col : col + P],
+                        in_=live["z", q][:, i, j * P : (j + 1) * P],
+                        identity=ident[:],
+                    )
+
+        def RL(q, js):
+            if not ok(q):
+                return
+            if js[0] == 0:
+                live["hp", q] = work.tile([P, 4, 2 * P], BF16, tag="hp", name="hp")
+            for j in js:
+                nc.scalar.activation(
+                    out=live["hp", q][:, j, :],
+                    in_=live["zt", q][j // 2][:, (j % 2) * 2 * P : (j % 2 + 1) * 2 * P],
+                    func=ACT.Relu,
+                    bias=gb1[:, 4 + j : 5 + j],
+                    scale=gb1[:, j : j + 1],
+                )
+
+        def RG(q):
+            if not ok(q):
+                return
+            hg = work.tile([P, 2 * P, 4], BF16, align_bytes=64, tag="hg", name="hg")
+            live["hg", q] = hg
+            nc.vector.tensor_copy(
+                out=hg[:].rearrange("p (c i) t -> p c t i", i=4),
+                in_=live["hp", q][:].rearrange("p t (c i) -> p c t i", i=4),
+            )
+
+        def HQ(q):
+            if not ok(q):
+                return
+            cols = slice(2 * q * P, (2 * q + 2) * P)
+            nc.vector.quantize_mx(
+                out=hcodes[:, cols].bitcast(FP8X4),
+                scales=hscales[:, cols],
+                in_=live["hg", q][:].rearrange("p k t -> p (k t)"),
+            )
+
+        def M2(q):
+            if not ok(q):
+                return
+            tag = ("ys", "ys", "yn", "zt", "zt", "ys", "yn", "zt")[q]
+            for i in range(2):
+                live["y2", q, i] = bank(tag, "y2")
+                mx(live["y2", q, i], hcodes, hscales, 2 * q + i, "w2")
+
+        def PA(q, i):
+            if not ok(q) or q in V_STATS:
+                return
+            if i == 0:
+                live["y2s", q] = work.tile([P, 2, D], F32, tag="y2s", name="y2s")
+                live["tot", q] = small.tile([P, 2], F32, tag="tot", name="tot")
+            nc.scalar.activation(
+                out=live["y2s", q][:, i, :],
+                in_=live["y2", q, i][:],
+                func=ACT.Identity,
+                accum_out=live["tot", q][:, i : i + 1],
+            )
+
+        def MU(q):
+            if not ok(q) or q in V_STATS:
+                return
+            negmu = small.tile([P, 2], F32, tag="negmu", name="negmu")
+            live["negmu", q] = negmu
+            nc.scalar.mul(out=negmu[:], in_=live["tot", q][:], mul=-1.0 / D)
+
+        def PB(q):
+            if not ok(q) or q in V_STATS:
+                return
+            ssq = small.tile([P, 2], F32, tag="ssq", name="ssq")
+            live["ssq", q] = ssq
+            for i in range(2):
+                junk = work.tile([P, D], BF16, tag="junk", bufs=2, name="junk")
+                nc.scalar.activation(
+                    out=junk[:],
+                    in_=live["y2s", q][:, i, :],
+                    func=ACT.Square,
+                    bias=live["negmu", q][:, i : i + 1],
+                    accum_out=ssq[:, i : i + 1],
+                )
+
+        def B2(q, i):
+            if ok(q) and q in V_STATS:
+                moments("b", q, i, "y2")
+
+        def A2(q, i):
+            if ok(q) and q in V_STATS:
+                aggregate("b", q, i)
+
+        def S2(q):
+            if not ok(q):
+                return
+            if q in V_STATS:
+                root("b", q, live["bmv", q][:, :, 1], 1)
+            else:
+                root("b", q, live["ssq", q][:], D)
+
+        def E2(q):
+            if ok(q):
+                add_eps("b", q)
+
+        def R2(q):
+            if ok(q):
+                invert("b", q)
+
+        def T1(q, i):
+            if not ok(q):
+                return
+            if i == 0:
+                live["t", q] = work.tile([P, 2, D], F32, tag="t", name="t")
+            if q in V_STATS:
+                nc.vector.scalar_tensor_tensor(
+                    out=live["t", q][:, i, :],
+                    in0=live["y2", q, i][:],
+                    scalar=live["bmv", q][:, i, 0:1],
+                    in1=gb2[:, 0, :],
+                    op0=ALU.subtract,
+                    op1=ALU.mult,
+                )
+            else:
+                nc.vector.scalar_tensor_tensor(
+                    out=live["t", q][:, i, :],
+                    in0=live["y2s", q][:, i, :],
+                    scalar=live["negmu", q][:, i : i + 1],
+                    in1=gb2[:, 0, :],
+                    op0=ALU.add,
+                    op1=ALU.mult,
+                )
+
+        def T2(q, i):
+            if not ok(q):
+                return
+            if i == 0:
+                live["o", q] = work.tile([P, 2, D], F32, tag="o", bufs=4, name="o")
+            o = live["o", q]
+            nc.vector.scalar_tensor_tensor(
+                out=o[:, i, :],
+                in0=live["t", q][:, i, :],
+                scalar=live["br", q][:, i : i + 1],
+                in1=gb2[:, 1, :],
+                op0=ALU.mult,
+                op1=ALU.add,
+            )
+            if q >= NP - 2:
+                nc.sync.dma_start(out=out[:, 2 * q + i, :], in_=o[:, i, :])
+            elif i == 1:
+                nc.sync.dma_start(out=out[:, 2 * q : 2 * q + 2, :], in_=o[:])
+
+        def late(n, i):
+            u = n - 6
+            if 0 <= u <= 3:
+                if u % 2 == 0:
+                    B2(u // 2, i)
+                else:
+                    T1(u // 2, i)
+
+        regroup_weight("w1", w1raw, 0, 256)
+        regroup_weight("w1", w1raw, 256, 512)
+        quantise_weight("w1", 0, 256)
+        quantise_weight("w1", 256, 512)
+        XT(0), XC(0), XT(1), XC(1), XQ(0), XT(2), XC(2), XT(3), XC(3), MS(0, 0), MS(0, 1), XQ(1)
+        XT(4), XC(4), XT(5), XC(5)
+        BN(0, 0), BN(0, 1), gains1_cast(), MS(1, 0), MS(1, 1), XT(6), XT(7)
+        XQ(2), AG(0, 0), XQ(3), AG(0, 1), SQ(0), XC(6)
+        BN(1, 0), E1(0), MN(0, 0), MN(0, 1), BN(1, 1), MS(2, 0), MS(2, 1)
+        R1(0), AG(1, 0), XQ(4), AG(1, 1), N1(0), XC(7), SQ(1)
+        BN(2, 0), BN(2, 1), MS(3, 0), MS(3, 1), E1(1), AG(2, 0)
+        regroup_weight("w2", w2raw, 0, 128)
+        R1(1), AG(2, 1)
+        regroup_weight("w2", w2raw, 128, 256)
+        N1(1)
+        NR(0, 0), NR(0, 1), SQ(2), MN(1, 0), MN(1, 1), ZT(0)
+        for n in range(1, NP + 3):
+            NR(n, 0), NR(n, 1)
+            BN(n + 2, 0), late(n, 0), MS(n + 3, 0), MN(n + 1, 0), MN(n + 1, 1), E1(n + 1)
+            if n == 8:
+                E2(0)
+            BN(n + 2, 1), late(n, 1), MS(n + 3, 1)
+            if n == 5:
+                M2(0)
+            if n == 7:
+                M2(1)
+            ZT(n), R1(n + 1)
+            if n == 8:
+                R2(0)
+            RG(n - 2)
+            if n == 1:
+                regroup_weight("w2", w2raw, 256, 384)
+            AG(n + 2, 0), AG(n + 2, 1)
+            if n == 6 or n == 8:
+                A2((n - 6) // 2, 0), A2((n - 6) // 2, 1)
+            N1(n + 1), HQ(n - 3)
+            if n <= 3:
+                XQ(n + 4)
+            if n == 2:
+                regroup_weight("w2", w2raw, 384, 512)
+            if n == 3:
+                quantise_weight("w2", 0, 256)
+            if n == 4:
+                quantise_weight("w2", 256, 512)
+            if n == 9:
+                T2(0, 0), T2(0, 1)
+            RL(n - 1, (0, 1, 2, 3)), SQ(n + 2)
+            if n == 7:
+                S2(0), M2(2)
+            if n == 8:
+                M2(3), M2(4)
+            if n == 9:
+                M2(5)
+        for k in range(2, NP + 1):
+            PA(k, 0)
+            if k == 3:
+                MU(2)
+            if k >= 3:
+                S2(k - 2)
+            PA(k, 1)
+            if k <= 3:
+                M2(k + 4)
+            if k >= 3:
+                PB(k - 1), MU(k)
+                E2(k - 2), T1(k - 1, 0), R2(k - 2), T1(k - 1, 1)
+                if k < NP:
+                    T2(k - 2, 0), T2(k - 2, 1)
+        S2(NP - 1), E2(NP - 1), T2(NP - 2, 0), R2(NP - 1), T2(NP - 2, 1), T2(NP - 1, 0), T2(NP - 1, 1)

@@ -18,7 +18,6 @@ EPS = 1e-9
 NP = S // 2
 FLOPS = 2 * 2 * (P * S) * D * D
 
-PINNED = True
 V_STATS = (0, 1)
 
 
@@ -31,8 +30,7 @@ def tile_rlstmcell_pa_kernel(
         work = ctx.enter_context(tc.tile_pool(name="work", bufs=3))
         small = ctx.enter_context(tc.tile_pool(name="small", bufs=5))
         psum = ctx.enter_context(tc.psum_pool(name="psum", bufs=2))
-        if PINNED:
-            ctx.enter_context(tc.manual_schedule())
+        ctx.enter_context(tc.manual_schedule())
 
         def bank(tag, name):
             return psum.tile([P, D], F32, tag=tag, bufs=(4 if tag == "zt" else 2), name=name)
@@ -44,14 +42,14 @@ def tile_rlstmcell_pa_kernel(
         make_identity(nc, ident[:])
 
         gb1raw = const.tile([P, 2, 16], BF16)
-        nc.scalar.dma_start(out=gb1raw[:, 0, 0:4], in_=mlp_gain_1.rearrange("(p t) -> p t", t=4))
-        nc.scalar.dma_start(out=gb1raw[:, 1, 0:4], in_=mlp_bias_1.rearrange("(p t) -> p t", t=4))
-        nc.scalar.sqrt(out=warm_out[:], in_=warm_in[:])
         w1raw = const.tile([P, 4, D], BF16)
-        nc.sync.dma_start(out=w1raw[:], in_=mlp_kernel_1.rearrange("(p j) c -> p j c", j=4))
+        nc.scalar.dma_start(out=w1raw[:], in_=mlp_kernel_1.rearrange("(p j) c -> p j c", j=4))
+        nc.scalar.sqrt(out=warm_out[:], in_=warm_in[:])
         x_all = const.tile([P, S, D], BF16)
         for lo, hi in ((0, 2), (2, 4), (4, 8), (8, 12), (12, 16)):
             nc.sync.dma_start(out=x_all[:, lo:hi, :], in_=c_att[:, lo:hi, :])
+        nc.sync.dma_start(out=gb1raw[:, 0, 0:4], in_=mlp_gain_1.rearrange("(p t) -> p t", t=4))
+        nc.sync.dma_start(out=gb1raw[:, 1, 0:4], in_=mlp_bias_1.rearrange("(p t) -> p t", t=4))
         w2raw = const.tile([P, 4, D], BF16)
         nc.sync.dma_start(out=w2raw[:], in_=mlp_kernel_2.rearrange("(p j) c -> p j c", j=4))
         gb2 = const.tile([P, 2, D], BF16)

from contextlib import ExitStack

import concourse.mybir as mybir
from concourse.masks import make_identity

F32 = mybir.dt.float32
BF16 = mybir.dt.bfloat16
U32 = mybir.dt.uint32
U8 = mybir.dt.uint8
FP8X4 = mybir.dt.float8_e4m3fn_x4
ACT = mybir.ActivationFunctionType
ALU = mybir.AluOpType

P = 128
S = 16
D = 512
EPS = 1e-9
NP = S // 2
FLOPS = 2 * 2 * (P * S) * D * D

V_STATS = (0, 1)


def tile_rlstmcell_pa_kernel(
    tc, c_att, mlp_kernel_1, mlp_kernel_2, mlp_gain_1, mlp_gain_2, mlp_bias_1, mlp_bias_2, out
):
    nc = tc.nc
    with ExitStack() as ctx:
        const = ctx.enter_context(tc.tile_pool(name="const", bufs=1))
        work = ctx.enter_context(tc.tile_pool(name="work", bufs=3))
        small = ctx.enter_context(tc.tile_pool(name="small", bufs=5))
        psum = ctx.enter_context(tc.psum_pool(name="psum", bufs=2))
        ctx.enter_context(tc.manual_schedule())

        def bank(tag, name):
            return psum.tile([P, D], F32, tag=tag, bufs=(4 if tag == "zt" else 2), name=name)

        warm_in = const.tile([P, 1], F32)
        warm_out = const.tile([P, 1], F32)
        nc.vector.memset(warm_in[:], 1.0)
        ident = const.tile([P, P], F32)
        make_identity(nc, ident[:])

        gb1raw = const.tile([P, 2, 16], BF16)
        w1raw = const.tile([P, 4, D], BF16)
        nc.scalar.dma_start(out=w1raw[:], in_=mlp_kernel_1.rearrange("(p j) c -> p j c", j=4))
        nc.scalar.sqrt(out=warm_out[:], in_=warm_in[:])
        x_all = const.tile([P, S, D], BF16)
        for lo, hi in ((0, 2), (2, 4), (4, 8), (8, 12), (12, 16)):
            nc.sync.dma_start(out=x_all[:, lo:hi, :], in_=c_att[:, lo:hi, :])
        nc.sync.dma_start(out=gb1raw[:, 0, 0:4], in_=mlp_gain_1.rearrange("(p t) -> p t", t=4))
        nc.sync.dma_start(out=gb1raw[:, 1, 0:4], in_=mlp_bias_1.rearrange("(p t) -> p t", t=4))
        w2raw = const.tile([P, 4, D], BF16)
        nc.sync.dma_start(out=w2raw[:], in_=mlp_kernel_2.rearrange("(p j) c -> p j c", j=4))
        gb2 = const.tile([P, 2, D], BF16)
        nc.sync.dma_start(out=gb2[:, 0, :], in_=mlp_gain_2.partition_broadcast(P))
        nc.sync.dma_start(out=gb2[:, 1, :], in_=mlp_bias_2.partition_broadcast(P))
        x_words = x_all[:].rearrange("p s d -> p (s d)").bitcast(F32)

        live = {}

        gb1 = const.tile([P, 8], F32)

        def gains1_cast():
            nc.vector.tensor_copy(out=gb1[:].rearrange("p (a t) -> p a t", a=2), in_=gb1raw[:, :, 0:4])

        wg = {}
        wcodes = {}
        wscales = {}
        for label in ("w1", "w2"):
            wg[label] = const.tile([P, D, 4], BF16, align_bytes=64, name=label + "_grouped")
            wcodes[label] = const.tile([P, D], U32, align_bytes=64, name=label + "_codes")
            wscales[label] = const.tile([P, D], U8, align_bytes=64, name=label + "_scales")
        xcodes = const.tile([P, S * P], U32, align_bytes=64)
        xscales = const.tile([P, S * P], U8, align_bytes=64)
        hcodes = const.tile([P, S * P], U32, align_bytes=64)
        hscales = const.tile([P, S * P], U8, align_bytes=64)

        def regroup_weight(label, raw, lo, hi):
            nc.vector.tensor_copy(
                out=wg[label][:, lo:hi, :].rearrange("p (c i) t -> p c t i", i=4),
                in_=raw[:, :, lo:hi].rearrange("p t (c i) -> p c t i", i=4),
            )

        def quantise_weight(label, lo, hi):
            nc.vector.quantize_mx(
                out=wcodes[label][:, lo:hi].bitcast(FP8X4),
                scales=wscales[label][:, lo:hi],
                in_=wg[label][:, lo:hi, :].rearrange("p c t -> p (c t)"),
            )

        def ok(q):
            return 0 <= q < NP

        def mx(dst, codes, scales, s, label):
            nc.tensor.matmul_mx(
                out=dst[:],
                lhsT=codes[:, s * P : (s + 1) * P].bitcast(FP8X4),
                lhsT_scale=scales[:, s * P : (s + 1) * P],
                rhs=wcodes[label][:].bitcast(FP8X4),
                rhs_scale=wscales[label][:],
                start=True,
                stop=True,
            )

        def XT(q):
            if not ok(q):
                return
            xt = bank("zt", "xt")
            live["xt", q] = xt
            for i in range(2):
                for u in range(2):
                    col = (2 * q + i) * 256 + u
                    nc.tensor.transpose(
                        out=xt[:, (2 * i + u) * P : (2 * i + u + 1) * P],
                        in_=x_words[:, col : col + 2 * P - 1 : 2],
                        identity=ident[:],
                    )

        def XC(q):
            if not ok(q):
                return
            xg = work.tile([P, 2 * D], BF16, align_bytes=64, tag="xg", bufs=4, name="xg")
            live["xg", q] = xg
            nc.scalar.copy(
                out=xg[:].bitcast(F32).rearrange("p (i k u) -> p i k u", i=2, u=2),
                in_=live["xt", q][:].rearrange("p (i u k) -> p i k u", i=2, u=2),
            )

        def XQ(q):
            if not ok(q):
                return
            cols = slice(2 * q * P, (2 * q + 2) * P)
            nc.vector.quantize_mx(out=xcodes[:, cols].bitcast(FP8X4), scales=xscales[:, cols], in_=live["xg", q][:])

        def MS(q, i):
            if ok(q):
                live["ys", q, i] = bank("ys", "ys")
                mx(live["ys", q, i], xcodes, xscales, 2 * q + i, "w1")

        def MN(q, i):
            if ok(q):
                live["yn", q, i] = bank("yn", "yn")
                mx(live["yn", q, i], xcodes, xscales, 2 * q + i, "w1")

        def moments(key, q, i, src):
            if i == 0:
                live[key + "st", q] = small.tile([P, 2, 6], F32, tag=key + "st", name=key + "st")
            nc.vector.bn_stats(out=live[key + "st", q][:, i, :], in_=live[src, q, i][:])

        def aggregate(key, q, i):
            if i == 0:
                live[key + "mv", q] = small.tile([P, 2, 2], F32, tag=key + "mv", name=key + "mv")
            nc.vector.bn_aggr(out=live[key + "mv", q][:, i, :], in_=live[key + "st", q][:, i, :])

        def BN(q, i):
            if ok(q):
                moments("a", q, i, "ys")

        def AG(q, i):
            if ok(q):
                aggregate("a", q, i)

        def root(key, q, src_ap, divisor):
            sd = small.tile([P, 2], F32, tag=key + "sd", name=key + "sd")
            live[key + "sd", q] = sd
            nc.scalar.activation(out=sd[:], in_=src_ap, func=ACT.Sqrt, scale=1.0 / divisor)

        def add_eps(key, q):
            sde = small.tile([P, 2], F32, tag=key + "sde", name=key + "sde")
            live[key + "sde", q] = sde
            nc.vector.tensor_scalar_add(out=sde[:], in0=live[key + "sd", q][:], scalar1=EPS)

        def invert(key, q):
            r = small.tile([P, 2], F32, tag=key + "r", name=key + "r")
            live[key + "r", q] = r
            nc.vector.reciprocal(out=r[:], in_=live[key + "sde", q][:])

        def SQ(q):
            if ok(q):
                root("a", q, live["amv", q][:, :, 1], 1)

        def E1(q):
            if ok(q):
                add_eps("a", q)

        def R1(q):
            if ok(q):
                invert("a", q)

        def N1(q):
            if not ok(q):
                return
            nmr = small.tile([P, 2], F32, tag="anmr", name="anmr")
            live["anmr", q] = nmr
            nc.vector.scalar_tensor_tensor(
                out=nmr[:], in0=live["amv", q][:, :, 0], scalar=-1.0, in1=live["ar", q][:], op0=ALU.mult, op1=ALU.mult
            )

        def NR(q, i):
            if not ok(q):
                return
            if i == 0:
                live["z", q] = work.tile([P, 2, D], F32, tag="z", name="z")
            nc.scalar.activation(
                out=live["z", q][:, i, :].rearrange("p (t m) -> p t m", t=4),
                in_=live["yn", q, i][:].rearrange("p (m t) -> p t m", t=4),
                func=ACT.Identity,
                bias=live["anmr", q][:, i : i + 1],
                scale=live["ar", q][:, i : i + 1],
            )

        def ZT(q):
            if not ok(q):
                return
            zts = [bank("zt", "zt"), bank("zt", "zt")]
            live["zt", q] = zts
            for i in range(2):
                for j in range(4):
                    col = (2 * (j % 2) + i) * P
                    nc.tensor.transpose(
                        out=zts[j // 2][:, col : col + P],
                        in_=live["z", q][:, i, j * P : (j + 1) * P],
                        identity=ident[:],
                    )

        def RL(q, js):
            if not ok(q):
                return
            if js[0] == 0:
                live["hp", q] = work.tile([P, 4, 2 * P], BF16, tag="hp", name="hp")
            for j in js:
                nc.scalar.activation(
                    out=live["hp", q][:, j, :],
                    in_=live["zt", q][j // 2][:, (j % 2) * 2 * P : (j % 2 + 1) * 2 * P],
                    func=ACT.Relu,
                    bias=gb1[:, 4 + j : 5 + j],
                    scale=gb1[:, j : j + 1],
                )

        def RG(q):
            if not ok(q):
                return
            hg = work.tile([P, 2 * P, 4], BF16, align_bytes=64, tag="hg", name="hg")
            live["hg", q] = hg
            nc.vector.tensor_copy(
                out=hg[:].rearrange("p (c i) t -> p c t i", i=4),
                in_=live["hp", q][:].rearrange("p t (c i) -> p c t i", i=4),
            )

        def HQ(q):
            if not ok(q):
                return
            cols = slice(2 * q * P, (2 * q + 2) * P)
            nc.vector.quantize_mx(
                out=hcodes[:, cols].bitcast(FP8X4),
                scales=hscales[:, cols],
                in_=live["hg", q][:].rearrange("p k t -> p (k t)"),
            )

        def M2(q):
            if not ok(q):
                return
            tag = ("ys", "ys", "yn", "zt", "zt", "ys", "yn", "zt")[q]
            for i in range(2):
                live["y2", q, i] = bank(tag, "y2")
                mx(live["y2", q, i], hcodes, hscales, 2 * q + i, "w2")

        def PA(q, i):
            if not ok(q) or q in V_STATS:
                return
            if i == 0:
                live["y2s", q] = work.tile([P, 2, D], F32, tag="y2s", name="y2s")
                live["tot", q] = small.tile([P, 2], F32, tag="tot", name="tot")
            nc.scalar.activation(
                out=live["y2s", q][:, i, :],
                in_=live["y2", q, i][:],
                func=ACT.Identity,
                accum_out=live["tot", q][:, i : i + 1],
            )

        def MU(q):
            if not ok(q) or q in V_STATS:
                return
            negmu = small.tile([P, 2], F32, tag="negmu", name="negmu")
            live["negmu", q] = negmu
            nc.scalar.mul(out=negmu[:], in_=live["tot", q][:], mul=-1.0 / D)

        def PB(q):
            if not ok(q) or q in V_STATS:
                return
            ssq = small.tile([P, 2], F32, tag="ssq", name="ssq")
            live["ssq", q] = ssq
            for i in range(2):
                junk = work.tile([P, D], BF16, tag="junk", bufs=2, name="junk")
                nc.scalar.activation(
                    out=junk[:],
                    in_=live["y2s", q][:, i, :],
                    func=ACT.Square,
                    bias=live["negmu", q][:, i : i + 1],
                    accum_out=ssq[:, i : i + 1],
                )

        def B2(q, i):
            if ok(q) and q in V_STATS:
                moments("b", q, i, "y2")

        def A2(q, i):
            if ok(q) and q in V_STATS:
                aggregate("b", q, i)

        def S2(q):
            if not ok(q):
                return
            if q in V_STATS:
                root("b", q, live["bmv", q][:, :, 1], 1)
            else:
                root("b", q, live["ssq", q][:], D)

        def E2(q):
            if ok(q):
                add_eps("b", q)

        def R2(q):
            if ok(q):
                invert("b", q)

        def T1(q, i):
            if not ok(q):
                return
            if i == 0:
                live["t", q] = work.tile([P, 2, D], F32, tag="t", name="t")
            if q in V_STATS:
                nc.vector.scalar_tensor_tensor(
                    out=live["t", q][:, i, :],
                    in0=live["y2", q, i][:],
                    scalar=live["bmv", q][:, i, 0:1],
                    in1=gb2[:, 0, :],
                    op0=ALU.subtract,
                    op1=ALU.mult,
                )
            else:
                nc.vector.scalar_tensor_tensor(
                    out=live["t", q][:, i, :],
                    in0=live["y2s", q][:, i, :],
                    scalar=live["negmu", q][:, i : i + 1],
                    in1=gb2[:, 0, :],
                    op0=ALU.add,
                    op1=ALU.mult,
                )

        def T2(q, i):
            if not ok(q):
                return
            if i == 0:
                live["o", q] = work.tile([P, 2, D], F32, tag="o", bufs=4, name="o")
            o = live["o", q]
            nc.vector.scalar_tensor_tensor(
                out=o[:, i, :],
                in0=live["t", q][:, i, :],
                scalar=live["br", q][:, i : i + 1],
                in1=gb2[:, 1, :],
                op0=ALU.mult,
                op1=ALU.add,
            )
            if q >= NP - 2:
                nc.sync.dma_start(out=out[:, 2 * q + i, :], in_=o[:, i, :])
            elif i == 1:
                nc.sync.dma_start(out=out[:, 2 * q : 2 * q + 2, :], in_=o[:])

        def late(n, i):
            u = n - 6
            if 0 <= u <= 3:
                if u % 2 == 0:
                    B2(u // 2, i)
                else:
                    T1(u // 2, i)

        regroup_weight("w1", w1raw, 0, 256)
        regroup_weight("w1", w1raw, 256, 512)
        quantise_weight("w1", 0, 256)
        quantise_weight("w1", 256, 512)
        XT(0), XC(0), XT(1), XC(1), XQ(0), XT(2), XC(2), XT(3), XC(3), MS(0, 0), MS(0, 1), XQ(1)
        XT(4), XC(4), XT(5), XC(5)
        BN(0, 0), BN(0, 1), gains1_cast(), MS(1, 0), MS(1, 1), XT(6), XT(7)
        XQ(2), AG(0, 0), XQ(3), AG(0, 1), SQ(0), XC(6)
        BN(1, 0), E1(0), MN(0, 0), MN(0, 1), BN(1, 1), MS(2, 0), MS(2, 1)
        R1(0), AG(1, 0), XQ(4), AG(1, 1), N1(0), XC(7), SQ(1)
        BN(2, 0), BN(2, 1), MS(3, 0), MS(3, 1), E1(1), AG(2, 0)
        regroup_weight("w2", w2raw, 0, 128)
        R1(1), AG(2, 1)
        regroup_weight("w2", w2raw, 128, 256)
        N1(1)
        NR(0, 0), NR(0, 1), SQ(2), MN(1, 0), MN(1, 1), ZT(0)
        for n in range(1, NP + 3):
            NR(n, 0), NR(n, 1)
            BN(n + 2, 0), late(n, 0), MS(n + 3, 0), MN(n + 1, 0), MN(n + 1, 1), E1(n + 1)
            if n == 8:
                E2(0)
            BN(n + 2, 1), late(n, 1), MS(n + 3, 1)
            if n == 5:
                M2(0)
            if n == 7:
                M2(1)
            ZT(n), R1(n + 1)
            if n == 8:
                R2(0)
            RG(n - 2)
            if n == 1:
                regroup_weight("w2", w2raw, 256, 384)
            AG(n + 2, 0), AG(n + 2, 1)
            if n == 6 or n == 8:
                A2((n - 6) // 2, 0), A2((n - 6) // 2, 1)
            N1(n + 1), HQ(n - 3)
            if n <= 3:
                XQ(n + 4)
            if n == 2:
                regroup_weight("w2", w2raw, 384, 512)
            if n == 3:
                quantise_weight("w2", 0, 256)
            if n == 4:
                quantise_weight("w2", 256, 512)
            if n == 9:
                T2(0, 0), T2(0, 1)
            RL(n - 1, (0, 1, 2, 3)), SQ(n + 2)
            if n == 7:
                S2(0), M2(2)
            if n == 8:
                M2(3), M2(4)
            if n == 9:
                M2(5)
        for k in range(2, NP + 1):
            PA(k, 0)
            if k == 3:
                MU(2)
            if k >= 3:
                S2(k - 2)
            PA(k, 1)
            if k <= 3:
                M2(k + 4)
            if k >= 3:
                PB(k - 1), MU(k)
                E2(k - 2), T1(k - 1, 0), R2(k - 2), T1(k - 1, 1)
                if k < NP:
                    T2(k - 2, 0), T2(k - 2, 1)
        S2(NP - 1), E2(NP - 1), T2(NP - 2, 0), R2(NP - 1), T2(NP - 2, 1), T2(NP - 1, 0), T2(NP - 1, 1)
